import numpy as np
import ml_dtypes


def mxq(x, axis, fmt="e4m3"):
    dtype, down = {"e4m3": (ml_dtypes.float8_e4m3fn, 7), "e5m2": (ml_dtypes.float8_e5m2, 14)}[fmt]
    v = np.moveaxis(np.asarray(x, np.float32).astype(ml_dtypes.bfloat16).astype(np.float64), axis, -1)
    blocks = v.reshape(v.shape[:-1] + (-1, 32))
    amax = np.abs(blocks).max(-1, keepdims=True)
    byte = np.maximum(np.where(amax > 0, np.frexp(amax)[1] - 1 + 127, 0) - down, 1)
    scale = np.exp2(byte - 127.0)
    codes = (blocks / scale).astype(np.float32).astype(dtype).astype(np.float64)
    return np.moveaxis((codes * scale).reshape(v.shape), -1, axis)


WIDE = False


def mx_kscale(k):
    if not WIDE:
        return np.ones(k)
    levels = np.array([10, -10, 5, -5, 0])
    a = np.random.permutation(np.resize(levels, k // 512 * 4)).reshape(k // 512, 4)
    idx = np.arange(k)
    return np.exp2(a[idx // 512, idx % 128 // 32])


BF16 = ml_dtypes.bfloat16


def bf(x):
    return np.asarray(x, np.float32).astype(BF16)


def f64(x):
    return np.asarray(x).astype(np.float64)


B, N, DIN, DH, DOUT = 256, 4, 512, 512, 512
EPS = 1e-5


def elu(v):
    return np.where(v > 0.0, v, np.expm1(np.minimum(v, 0.0)))


def sigmoid(v):
    return 1.0 / (1.0 + np.exp(-v))


def setup_inputs():
    rn = np.random.standard_normal
    s, t = mx_kscale(DH), mx_kscale(DOUT)
    z = rn((B, N, DOUT))
    e = np.exp(z - z.max(1, keepdims=True))
    return {
        "hv": bf(elu(rn((B, N, DH))) * s),
        "x": bf(rn((B, N, DIN)) + 0.5),
        "sel_w": bf(e / e.sum(1, keepdims=True)),
        "vW1": bf(rn((N, DH, DOUT)) * 1.2 / np.sqrt(DH) / s[:, None] * t),
        "vb1": bf(rn((N, DOUT)) * 0.3 * t),
        "vW4": bf(rn((N, DOUT, DOUT)) / np.sqrt(DOUT) / t[:, None]),
        "vb4": bf(rn((N, DOUT)) * 0.3),
        "vW5": bf(rn((N, DOUT, DOUT)) / np.sqrt(DOUT) / t[:, None]),
        "vb5": bf(rn((N, DOUT)) * 0.3),
        "vlng": bf(1.0 + 0.2 * rn((N, DOUT))),
        "vlnb": bf(0.2 * rn((N, DOUT))),
    }


def reference(hv, x, sel_w, vW1, vb1, vW4, vb4, vW5, vb5, vlng, vlnb):
    hq = mxq(f64(hv).transpose(1, 0, 2), 2, "e4m3")
    e1v = (hq @ mxq(f64(vW1), 1, "e4m3")) + f64(vb1)[:, None, :]
    eq = mxq(e1v, 2, "e4m3")
    gv = sigmoid((eq @ mxq(f64(vW4), 1, "e4m3")) + f64(vb4)[:, None, :]) * ((eq @ mxq(f64(vW5), 1, "e4m3")) + f64(vb5)[:, None, :])
    r = f64(x) + gv.transpose(1, 0, 2)
    yv = (r - r.mean(-1, keepdims=True)) * (1.0 / np.sqrt(r.var(-1, keepdims=True) + EPS)) * f64(vlng) + f64(vlnb)
    return np.sum(f64(sel_w) * yv, axis=1)

@@ -1,0 +1,311 @@
+from contextlib import ExitStack
+
+import concourse.mybir as mybir
+from concourse.masks import make_identity
+
+F32 = mybir.dt.float32
+BF16 = mybir.dt.bfloat16
+U32 = mybir.dt.uint32
+U8 = mybir.dt.uint8
+FP8X4 = mybir.dt.float8_e4m3fn_x4
+ALU = mybir.AluOpType
+ACT = mybir.ActivationFunctionType
+
+P = 128
+PACK = 4
+B = 256
+NV = 4
+D = 512
+HALVES = B // P
+CHUNKS = D // P
+EPS = 1e-5
+
+FLOPS = 3 * NV * 2 * B * D * D
+
+
+def tile_variableselectionnetwork_pb_kernel(
+    tc, hv, x, sel_w, vW1, vb1, vW4, vb4, vW5, vb5, vlng, vlnb, out
+):
+    nc = tc.nc
+    with ExitStack() as ctx:
+        consts = ctx.enter_context(tc.tile_pool(name="consts", bufs=1))
+        loads = ctx.enter_context(tc.tile_pool(name="loads", bufs=1))
+        quantised = ctx.enter_context(tc.tile_pool(name="quantised", bufs=1))
+        staging = ctx.enter_context(tc.tile_pool(name="staging", bufs=3))
+        work = ctx.enter_context(tc.tile_pool(name="work", bufs=4))
+        psum_stage1 = ctx.enter_context(tc.psum_pool(name="psum_stage1", bufs=2))
+        psum_gate = ctx.enter_context(tc.psum_pool(name="psum_gate", bufs=4))
+        psum_rows = ctx.enter_context(tc.psum_pool(name="psum_rows", bufs=2))
+
+        bias_rows = consts.tile([P, P], BF16)
+        nc.vector.memset(bias_rows[:], 0.0)
+        for i, vec in enumerate((vb1, vb4, vb5)):
+            nc.scalar.dma_start(
+                out=bias_rows[NV * CHUNKS * i : NV * CHUNKS * (i + 1), :],
+                in_=vec.rearrange("n (c p) -> (n c) p", p=P),
+            )
+
+        def load_rows(src, name):
+            tiles = []
+            for h in range(HALVES):
+                t = loads.tile([P, NV * D], BF16, name="%s%d" % (name, h))
+                nc.sync.dma_start(
+                    out=t[:], in_=src[h * P : (h + 1) * P].rearrange("b n d -> b (n d)")
+                )
+                tiles.append(t)
+            return tiles
+
+        def load_w1(n):
+            t = loads.tile([P, PACK, D], BF16, name="w1_raw%d" % n)
+            nc.sync.dma_start(
+                out=t[:].rearrange("q (u e) c -> q u e c", u=2),
+                in_=vW1[n].rearrange("(u q e) c -> q u e c", u=2, e=2),
+            )
+            return t
+
+        def load_w45(w, n, name):
+            t = loads.tile([P, PACK, D], BF16, name="%s_raw%d" % (name, n))
+            nc.sync.dma_start(out=t[:], in_=w[n].rearrange("(t p) c -> p t c", p=P))
+            return t
+
+        def load_broadcast(vec, name):
+            t = loads.tile([P, NV * D], BF16, name=name)
+            nc.sync.dma_start(out=t[:], in_=vec.rearrange("n d -> (n d)").partition_broadcast(P))
+            return t
+
+        w1_raw, w4_raw, w5_raw = {}, {}, {}
+        w1_raw[0] = load_w1(0)
+        hv_sb = load_rows(hv, "hv")
+        w4_raw[0] = load_w45(vW4, 0, "w4")
+        w5_raw[0] = load_w45(vW5, 0, "w5")
+        w1_raw[1] = load_w1(1)
+        w4_raw[1] = load_w45(vW4, 1, "w4")
+        w5_raw[1] = load_w45(vW5, 1, "w5")
+        x_sb = load_rows(x, "x")
+        gamma_bc = load_broadcast(vlng, "gamma_bc")
+        beta_bc = load_broadcast(vlnb, "beta_bc")
+        sel_sb = load_rows(sel_w, "sel")
+        for n in range(2, NV):
+            w1_raw[n] = load_w1(n)
+            w4_raw[n] = load_w45(vW4, n, "w4")
+            w5_raw[n] = load_w45(vW5, n, "w5")
+
+        ident = consts.tile([P, P], F32)
+        make_identity(nc, ident[:])
+        minus_half = consts.tile([P, HALVES], F32)
+        nc.gpsimd.memset(minus_half[:], -0.5)
+
+        table_warm = consts.tile([P, 1], F32)
+        nc.scalar.activation(out=table_warm[:], in_=minus_half[:, 0:1], func=ACT.Sigmoid)
+
+        bias_rows_f32 = consts.tile([P, P], F32)
+        nc.vector.tensor_copy(out=bias_rows_f32[:], in_=bias_rows[:])
+        bias_ps = psum_stage1.tile([P, P], F32, tag="stage1")
+        nc.tensor.transpose(bias_ps[:], bias_rows_f32[:], ident[:])
+        bias_cols = consts.tile([P, P], F32)
+        nc.vector.tensor_copy(out=bias_cols[:], in_=bias_ps[:])
+
+        def bias_col(i, n, c):
+            j = NV * CHUNKS * i + CHUNKS * n + c
+            return bias_cols[:, j : j + 1]
+
+        row_sum = consts.tile([P, NV * HALVES], F32)
+        sq_sum = consts.tile([P, NV * HALVES], F32)
+        neg_mean = consts.tile([P, NV * HALVES], F32)
+        var_eps = consts.tile([P, NV * HALVES], F32)
+        rstd = consts.tile([P, NV * HALVES], F32)
+
+        acc = [consts.tile([P, D], F32, name="acc%d" % h) for h in range(HALVES)]
+
+        def quantise_weight(raw, name, n):
+            grouped = staging.tile([P, D, PACK], BF16, tag="grouped", align_bytes=64)
+            dst = grouped[:].rearrange("p (c i) t -> p c t i", i=4)
+            src = raw[:].rearrange("p t (c i) -> p c t i", i=4)
+            if n == 0:
+                nc.vector.tensor_copy(out=dst, in_=src)
+            else:
+                nc.scalar.copy(out=dst, in_=src)
+            codes = quantised.tile([P, D], U32, name="%s_codes%d" % (name, n), align_bytes=64)
+            scales = quantised.tile([P, D], U8, name="%s_scales%d" % (name, n), align_bytes=64)
+            nc.vector.quantize_mx(
+                out=codes[:].bitcast(FP8X4),
+                scales=scales[:],
+                in_=grouped[:].rearrange("p c t -> p (c t)"),
+            )
+            return codes, scales
+
+        def quantise_hv(n):
+            words_per_row = D // 2
+            hvT_ps = psum_stage1.tile([P, 2, B], F32, tag="stage1")
+            for u in range(2):
+                for h in range(HALVES):
+                    first = n * words_per_row + u * P
+                    nc.tensor.transpose(
+                        hvT_ps[:, u, h * P : (h + 1) * P],
+                        hv_sb[h][:].bitcast(F32)[:, first : first + P],
+                        ident[:],
+                    )
+            grouped = staging.tile([P, B * PACK], BF16, tag="hv_grouped", align_bytes=64)
+            nc.scalar.copy(
+                out=grouped[:].bitcast(F32).rearrange("p (b u) -> p b u", u=2),
+                in_=hvT_ps[:].rearrange("p u b -> p b u"),
+            )
+            codes = quantised.tile([P, B], U32, name="hv_codes%d" % n, align_bytes=64)
+            scales = quantised.tile([P, B], U8, name="hv_scales%d" % n, align_bytes=64)
+            nc.vector.quantize_mx(out=codes[:].bitcast(FP8X4), scales=scales[:], in_=grouped[:])
+            return codes, scales
+
+        def first_product(n, w1_q, hv_q):
+            grouped = staging.tile([P, B, PACK], BF16, tag="e1_grouped", align_bytes=64)
+            for h in range(HALVES):
+                rows = slice(h * P, (h + 1) * P)
+                e1_ps = psum_stage1.tile([P, PACK, P], F32, tag="stage1")
+                for t in range(PACK):
+                    feats = slice(t * P, (t + 1) * P)
+                    nc.tensor.matmul_mx(
+                        out=e1_ps[:, t, :],
+                        lhsT=w1_q[0][:, feats].bitcast(FP8X4),
+                        lhsT_scale=w1_q[1][:, feats],
+                        rhs=hv_q[0][:, rows].bitcast(FP8X4),
+                        rhs_scale=hv_q[1][:, rows],
+                        start=True,
+                        stop=True,
+                    )
+                first = CHUNKS * n
+                nc.vector.tensor_tensor(
+                    out=grouped[:, rows, :],
+                    in0=e1_ps[:].rearrange("p t b -> p b t"),
+                    in1=bias_cols[:, first : first + PACK].unsqueeze(1).to_broadcast([P, P, PACK]),
+                    op=ALU.add,
+                )
+            codes = staging.tile([P, B], U32, tag="e1_codes", align_bytes=64)
+            scales = staging.tile([P, B], U8, tag="e1_scales", align_bytes=64)
+            nc.vector.quantize_mx(
+                out=codes[:].bitcast(FP8X4),
+                scales=scales[:],
+                in_=grouped[:].rearrange("p b t -> p (b t)"),
+            )
+            return codes, scales
+
+        def gate(n, e1_q, w4_q, w5_q):
+            gvT = work.tile([P, CHUNKS, B], F32, tag="gvT", bufs=2)
+            for pair in range(CHUNKS // 2):
+                banks = []
+                for w_q in (w4_q, w5_q):
+                    g_ps = psum_gate.tile([P, 2, B], F32, tag="gate")
+                    for i in range(2):
+                        c = 2 * pair + i
+                        feats = slice(c * P, (c + 1) * P)
+                        nc.tensor.matmul_mx(
+                            out=g_ps[:, i, :],
+                            lhsT=w_q[0][:, feats].bitcast(FP8X4),
+                            lhsT_scale=w_q[1][:, feats],
+                            rhs=e1_q[0][:].bitcast(FP8X4),
+                            rhs_scale=e1_q[1][:],
+                            start=True,
+                            stop=True,
+                        )
+                    banks.append(g_ps)
+                sig = work.tile([P, 2, B], F32, tag="sig")
+                for i in range(2):
+                    c = 2 * pair + i
+                    nc.scalar.activation(
+                        out=sig[:, i, :], in_=banks[0][:, i, :], func=ACT.Sigmoid, bias=bias_col(1, n, c)
+                    )
+                    nc.vector.scalar_tensor_tensor(
+                        out=gvT[:, c, :],
+                        in0=banks[1][:, i, :],
+                        scalar=bias_col(2, n, c),
+                        in1=sig[:, i, :],
+                        op0=ALU.add,
+                        op1=ALU.mult,
+                    )
+            return gvT
+
+        def residual_and_statistics(n, gvT):
+            feats = slice(n * D, (n + 1) * D)
+            cols = slice(n * HALVES, (n + 1) * HALVES)
+            r = []
+            for h in range(HALVES):
+                gv_ps = psum_rows.tile([P, D], F32, tag="gv")
+                for c in range(CHUNKS):
+                    nc.tensor.transpose(
+                        gv_ps[:, c * P : (c + 1) * P], gvT[:, c, h * P : (h + 1) * P], ident[:]
+                    )
+                r_h = work.tile([P, D], F32, tag="r", bufs=2 * HALVES + 1)
+                j = n * HALVES + h
+                nc.vector.scalar_tensor_tensor(
+                    out=r_h[:],
+                    in0=gv_ps[:],
+                    scalar=1.0,
+                    in1=x_sb[h][:, feats],
+                    op0=ALU.mult,
+                    op1=ALU.add,
+                    accum_out=row_sum[:, j : j + 1],
+                )
+                r.append(r_h)
+            nc.gpsimd.tensor_scalar(
+                out=neg_mean[:, cols], in0=row_sum[:, cols],
+                scalar1=-1.0 / D, scalar2=0.0, op0=ALU.mult, op1=ALU.add,
+            )
+            for h in range(HALVES):
+                j = n * HALVES + h
+                squares = work.tile([P, D], BF16, tag="squares")
+                nc.scalar.activation(
+                    out=squares[:], in_=r[h][:], func=ACT.Square,
+                    bias=neg_mean[:, j : j + 1], accum_out=sq_sum[:, j : j + 1],
+                )
+            nc.gpsimd.tensor_scalar(
+                out=var_eps[:, cols], in0=sq_sum[:, cols],
+                scalar1=1.0 / D, scalar2=EPS, op0=ALU.mult, op1=ALU.add,
+            )
+            nc.gpsimd.tensor_tensor(
+                out=rstd[:, cols], in0=var_eps[:, cols], in1=minus_half[:], op=ALU.pow
+            )
+            return r
+
+        def normalise_and_add(n, r):
+            feats = slice(n * D, (n + 1) * D)
+            scaled, y, weighted = [], [], []
+            for h in range(HALVES):
+                j = n * HALVES + h
+                t = work.tile([P, D], F32, tag="scaled")
+                nc.vector.scalar_tensor_tensor(
+                    out=t[:], in0=r[h][:], scalar=neg_mean[:, j : j + 1], in1=gamma_bc[:, feats],
+                    op0=ALU.add, op1=ALU.mult,
+                )
+                scaled.append(t)
+            for h in range(HALVES):
+                j = n * HALVES + h
+                t = work.tile([P, D], F32, tag="y")
+                nc.vector.scalar_tensor_tensor(
+                    out=t[:], in0=scaled[h][:], scalar=rstd[:, j : j + 1], in1=beta_bc[:, feats],
+                    op0=ALU.mult, op1=ALU.add,
+                )
+                y.append(t)
+            for h in range(HALVES):
+                t = acc[h] if n == 0 else work.tile([P, D], F32, name="weighted", tag="weighted")
+                nc.vector.tensor_tensor(out=t[:], in0=y[h][:], in1=sel_sb[h][:, feats], op=ALU.mult)
+                weighted.append(t)
+            if n > 0:
+                for h in range(HALVES):
+                    nc.vector.tensor_tensor(
+                        out=acc[h][:], in0=acc[h][:], in1=weighted[h][:], op=ALU.add
+                    )
+
+        hv_q = [quantise_hv(n) for n in range(NV)]
+        r_before = None
+        for n in range(NV):
+            w1_q = quantise_weight(w1_raw[n], "w1", n)
+            e1_q = first_product(n, w1_q, hv_q[n])
+            w4_q = quantise_weight(w4_raw[n], "w4", n)
+            w5_q = quantise_weight(w5_raw[n], "w5", n)
+            gvT = gate(n, e1_q, w4_q, w5_q)
+            r = residual_and_statistics(n, gvT)
+            if n > 0:
+                normalise_and_add(n - 1, r_before)
+            r_before = r
+        normalise_and_add(NV - 1, r_before)
+
+        for h in range(HALVES):
+            nc.sync.dma_start(out=out[h * P : (h + 1) * P, :], in_=acc[h][:])

@@ -39,11 +39,13 @@ def tile_variableselectionnetwork_pb_kernel(
 
         bias_rows = consts.tile([P, P], BF16)
         nc.vector.memset(bias_rows[:], 0.0)
-        for i, vec in enumerate((vb1, vb4, vb5)):
-            nc.scalar.dma_start(
-                out=bias_rows[NV * CHUNKS * i : NV * CHUNKS * (i + 1), :],
-                in_=vec.rearrange("n (c p) -> (n c) p", p=P),
-            )
+
+        def load_bias_rows():
+            for i, vec in enumerate((vb1, vb4, vb5)):
+                nc.sync.dma_start(
+                    out=bias_rows[NV * CHUNKS * i : NV * CHUNKS * (i + 1), :],
+                    in_=vec.rearrange("n (c p) -> (n c) p", p=P),
+                )
 
         def load_rows(src, name):
             tiles = []
@@ -76,34 +78,34 @@ def tile_variableselectionnetwork_pb_kernel(
         w1_raw, w4_raw, w5_raw = {}, {}, {}
         w1_raw[0] = load_w1(0)
         hv_sb = load_rows(hv, "hv")
+        load_bias_rows()
         w4_raw[0] = load_w45(vW4, 0, "w4")
         w5_raw[0] = load_w45(vW5, 0, "w5")
         w1_raw[1] = load_w1(1)
         w4_raw[1] = load_w45(vW4, 1, "w4")
         w5_raw[1] = load_w45(vW5, 1, "w5")
+        w1_raw[2] = load_w1(2)
         x_sb = load_rows(x, "x")
+        w4_raw[2] = load_w45(vW4, 2, "w4")
+        w5_raw[2] = load_w45(vW5, 2, "w5")
         gamma_bc = load_broadcast(vlng, "gamma_bc")
         beta_bc = load_broadcast(vlnb, "beta_bc")
         sel_sb = load_rows(sel_w, "sel")
-        for n in range(2, NV):
-            w1_raw[n] = load_w1(n)
-            w4_raw[n] = load_w45(vW4, n, "w4")
-            w5_raw[n] = load_w45(vW5, n, "w5")
+        w1_raw[3] = load_w1(3)
+        w4_raw[3] = load_w45(vW4, 3, "w4")
+        w5_raw[3] = load_w45(vW5, 3, "w5")
 
         ident = consts.tile([P, P], F32)
         make_identity(nc, ident[:])
+        ident_bf16 = consts.tile([P, P], BF16)
+        make_identity(nc, ident_bf16[:])
         minus_half = consts.tile([P, HALVES], F32)
         nc.gpsimd.memset(minus_half[:], -0.5)
 
         table_warm = consts.tile([P, 1], F32)
         nc.scalar.activation(out=table_warm[:], in_=minus_half[:, 0:1], func=ACT.Sigmoid)
 
-        bias_rows_f32 = consts.tile([P, P], F32)
-        nc.vector.tensor_copy(out=bias_rows_f32[:], in_=bias_rows[:])
-        bias_ps = psum_stage1.tile([P, P], F32, tag="stage1")
-        nc.tensor.transpose(bias_ps[:], bias_rows_f32[:], ident[:])
         bias_cols = consts.tile([P, P], F32)
-        nc.vector.tensor_copy(out=bias_cols[:], in_=bias_ps[:])
 
         def bias_col(i, n, c):
             j = NV * CHUNKS * i + CHUNKS * n + c
@@ -121,7 +123,7 @@ def tile_variableselectionnetwork_pb_kernel(
             grouped = staging.tile([P, D, PACK], BF16, tag="grouped", align_bytes=64)
             dst = grouped[:].rearrange("p (c i) t -> p c t i", i=4)
             src = raw[:].rearrange("p t (c i) -> p c t i", i=4)
-            if n == 0:
+            if n == 0 or name == "w1":
                 nc.vector.tensor_copy(out=dst, in_=src)
             else:
                 nc.scalar.copy(out=dst, in_=src)
@@ -227,21 +229,23 @@ def tile_variableselectionnetwork_pb_kernel(
             cols = slice(n * HALVES, (n + 1) * HALVES)
             r = []
             for h in range(HALVES):
-                gv_ps = psum_rows.tile([P, D], F32, tag="gv")
+                r_ps = psum_rows.tile([P, D], F32, tag="r_ps")
+                nc.tensor.matmul(
+                    out=r_ps[:], lhsT=ident_bf16[:], rhs=x_sb[h][:, feats], start=True, stop=False
+                )
                 for c in range(CHUNKS):
-                    nc.tensor.transpose(
-                        gv_ps[:, c * P : (c + 1) * P], gvT[:, c, h * P : (h + 1) * P], ident[:]
+                    nc.tensor.matmul(
+                        out=r_ps[:, c * P : (c + 1) * P],
+                        lhsT=gvT[:, c, h * P : (h + 1) * P],
+                        rhs=ident[:],
+                        is_transpose=True,
+                        start=False,
+                        stop=(c == CHUNKS - 1),
                     )
-                r_h = work.tile([P, D], F32, tag="r", bufs=2 * HALVES + 1)
+                r_h = work.tile([P, D], F32, tag="r", bufs=NV * HALVES)
                 j = n * HALVES + h
-                nc.vector.scalar_tensor_tensor(
-                    out=r_h[:],
-                    in0=gv_ps[:],
-                    scalar=1.0,
-                    in1=x_sb[h][:, feats],
-                    op0=ALU.mult,
-                    op1=ALU.add,
-                    accum_out=row_sum[:, j : j + 1],
+                nc.scalar.activation(
+                    out=r_h[:], in_=r_ps[:], func=ACT.Identity, accum_out=row_sum[:, j : j + 1]
                 )
                 r.append(r_h)
             nc.gpsimd.tensor_scalar(
@@ -294,18 +298,21 @@ def tile_variableselectionnetwork_pb_kernel(
                     )
 
         hv_q = [quantise_hv(n) for n in range(NV)]
-        r_before = None
+        bias_rows_f32 = consts.tile([P, P], F32)
+        nc.vector.tensor_copy(out=bias_rows_f32[:], in_=bias_rows[:])
+        bias_ps = psum_stage1.tile([P, P], F32, tag="stage1")
+        nc.tensor.transpose(bias_ps[:], bias_rows_f32[:], ident[:])
+        nc.vector.tensor_copy(out=bias_cols[:], in_=bias_ps[:])
+        r = []
         for n in range(NV):
             w1_q = quantise_weight(w1_raw[n], "w1", n)
             e1_q = first_product(n, w1_q, hv_q[n])
             w4_q = quantise_weight(w4_raw[n], "w4", n)
             w5_q = quantise_weight(w5_raw[n], "w5", n)
             gvT = gate(n, e1_q, w4_q, w5_q)
-            r = residual_and_statistics(n, gvT)
-            if n > 0:
-                normalise_and_add(n - 1, r_before)
-            r_before = r
-        normalise_and_add(NV - 1, r_before)
+            r.append(residual_and_statistics(n, gvT))
+        for n in range(NV):
+            normalise_and_add(n, r[n])
 
         for h in range(HALVES):
             nc.sync.dma_start(out=out[h * P : (h + 1) * P, :], in_=acc[h][:])

@@ -19,6 +19,8 @@ D = 512
 HALVES = B // P
 CHUNKS = D // P
 EPS = 1e-5
+BIAS_VECTORS = 3
+NORM_VECTORS = 2
 
 FLOPS = 3 * NV * 2 * B * D * D
 
@@ -41,7 +43,7 @@ def tile_variableselectionnetwork_pb_kernel(
         nc.vector.memset(bias_rows[:], 0.0)
 
         def load_bias_rows():
-            for i, vec in enumerate((vb1, vb4, vb5)):
+            for i, vec in enumerate((vb1, vb4, vb5, vlng, vlnb)):
                 nc.sync.dma_start(
                     out=bias_rows[NV * CHUNKS * i : NV * CHUNKS * (i + 1), :],
                     in_=vec.rearrange("n (c p) -> (n c) p", p=P),
@@ -70,15 +72,10 @@ def tile_variableselectionnetwork_pb_kernel(
             nc.sync.dma_start(out=t[:], in_=w[n].rearrange("(t p) c -> p t c", p=P))
             return t
 
-        def load_broadcast(vec, name):
-            t = loads.tile([P, NV * D], BF16, name=name)
-            nc.sync.dma_start(out=t[:], in_=vec.rearrange("n d -> (n d)").partition_broadcast(P))
-            return t
-
         w1_raw, w4_raw, w5_raw = {}, {}, {}
+        load_bias_rows()
         w1_raw[0] = load_w1(0)
         hv_sb = load_rows(hv, "hv")
-        load_bias_rows()
         w4_raw[0] = load_w45(vW4, 0, "w4")
         w5_raw[0] = load_w45(vW5, 0, "w5")
         w1_raw[1] = load_w1(1)
@@ -88,8 +85,6 @@ def tile_variableselectionnetwork_pb_kernel(
         x_sb = load_rows(x, "x")
         w4_raw[2] = load_w45(vW4, 2, "w4")
         w5_raw[2] = load_w45(vW5, 2, "w5")
-        gamma_bc = load_broadcast(vlng, "gamma_bc")
-        beta_bc = load_broadcast(vlnb, "beta_bc")
         sel_sb = load_rows(sel_w, "sel")
         w1_raw[3] = load_w1(3)
         w4_raw[3] = load_w45(vW4, 3, "w4")
@@ -105,11 +100,27 @@ def tile_variableselectionnetwork_pb_kernel(
         table_warm = consts.tile([P, 1], F32)
         nc.scalar.activation(out=table_warm[:], in_=minus_half[:, 0:1], func=ACT.Sigmoid)
 
-        bias_cols = consts.tile([P, P], F32)
+        bias_cols = consts.tile([P, BIAS_VECTORS * NV * CHUNKS], F32)
+        norm_cols = consts.tile([P, NORM_VECTORS * NV * CHUNKS], BF16)
 
         def bias_col(i, n, c):
             j = NV * CHUNKS * i + CHUNKS * n + c
             return bias_cols[:, j : j + 1]
+
+        def spread_over_partitions(i, name):
+            spread = consts.tile([P, NV * D], BF16, name=name)
+            blocks_per_bank = 2 * D // P
+            for bank in range(NV * CHUNKS // blocks_per_bank):
+                spread_ps = psum_gate.tile([P, 2 * D], BF16, tag="gate")
+                for b in range(blocks_per_bank):
+                    j = NV * CHUNKS * i + blocks_per_bank * bank + b
+                    nc.tensor.transpose(
+                        spread_ps[:, b * P : (b + 1) * P],
+                        norm_cols[:, j : j + 1].to_broadcast([P, P]),
+                        ident_bf16[:],
+                    )
+                nc.scalar.copy(out=spread[:, bank * 2 * D : (bank + 1) * 2 * D], in_=spread_ps[:])
+            return spread
 
         row_sum = consts.tile([P, NV * HALVES], F32)
         sq_sum = consts.tile([P, NV * HALVES], F32)
@@ -297,20 +308,28 @@ def tile_variableselectionnetwork_pb_kernel(
                         out=acc[h][:], in0=acc[h][:], in1=weighted[h][:], op=ALU.add
                     )
 
-        hv_q = [quantise_hv(n) for n in range(NV)]
-        bias_rows_f32 = consts.tile([P, P], F32)
-        nc.vector.tensor_copy(out=bias_rows_f32[:], in_=bias_rows[:])
-        bias_ps = psum_stage1.tile([P, P], F32, tag="stage1")
-        nc.tensor.transpose(bias_ps[:], bias_rows_f32[:], ident[:])
-        nc.vector.tensor_copy(out=bias_cols[:], in_=bias_ps[:])
-        r = []
-        for n in range(NV):
+        def products_and_statistics(n):
             w1_q = quantise_weight(w1_raw[n], "w1", n)
             e1_q = first_product(n, w1_q, hv_q[n])
             w4_q = quantise_weight(w4_raw[n], "w4", n)
             w5_q = quantise_weight(w5_raw[n], "w5", n)
             gvT = gate(n, e1_q, w4_q, w5_q)
-            r.append(residual_and_statistics(n, gvT))
+            return residual_and_statistics(n, gvT)
+
+        cols_ps = psum_stage1.tile([P, P], BF16, tag="stage1")
+        nc.tensor.transpose(cols_ps[:], bias_rows[:], ident_bf16[:])
+        first_norm_col = BIAS_VECTORS * NV * CHUNKS
+        nc.vector.tensor_copy(out=bias_cols[:], in_=cols_ps[:, 0:first_norm_col])
+        nc.vector.tensor_copy(
+            out=norm_cols[:],
+            in_=cols_ps[:, first_norm_col : first_norm_col + NORM_VECTORS * NV * CHUNKS],
+        )
+        hv_q = [quantise_hv(n) for n in range(NV)]
+        r = [products_and_statistics(0)]
+        gamma_bc = spread_over_partitions(0, "gamma_bc")
+        beta_bc = spread_over_partitions(1, "beta_bc")
+        for n in range(1, NV):
+            r.append(products_and_statistics(n))
         for n in range(NV):
             normalise_and_add(n, r[n])
 

@@ -19,8 +19,12 @@ D = 512
 HALVES = B // P
 CHUNKS = D // P
 EPS = 1e-5
-BIAS_VECTORS = 3
-NORM_VECTORS = 2
+VB1 = 0
+VB4 = 1
+VB5 = 2
+VLNG = 3
+VLNB = 4
+VECTOR_COLS = 256
 
 FLOPS = 3 * NV * 2 * B * D * D
 
@@ -36,28 +40,25 @@ def tile_variableselectionnetwork_pb_kernel(
         staging = ctx.enter_context(tc.tile_pool(name="staging", bufs=3))
         work = ctx.enter_context(tc.tile_pool(name="work", bufs=4))
         psum_stage1 = ctx.enter_context(tc.psum_pool(name="psum_stage1", bufs=2))
-        psum_gate = ctx.enter_context(tc.psum_pool(name="psum_gate", bufs=4))
+        psum_gate = ctx.enter_context(tc.psum_pool(name="psum_gate", bufs=2))
         psum_rows = ctx.enter_context(tc.psum_pool(name="psum_rows", bufs=2))
+        psum_out = ctx.enter_context(tc.psum_pool(name="psum_out", bufs=1))
 
-        bias_rows = consts.tile([P, P], BF16)
-        nc.vector.memset(bias_rows[:], 0.0)
+        vector_rows = consts.tile([P, P], BF16)
+        nc.vector.memset(vector_rows[:], 0.0)
+        for i, vec in enumerate((vb1, vb4, vb5, vlng, vlnb)):
+            nc.sync.dma_start(
+                out=vector_rows[NV * CHUNKS * i : NV * CHUNKS * (i + 1), :],
+                in_=vec.rearrange("n (c p) -> (n c) p", p=P),
+            )
 
-        def load_bias_rows():
-            for i, vec in enumerate((vb1, vb4, vb5, vlng, vlnb)):
-                nc.sync.dma_start(
-                    out=bias_rows[NV * CHUNKS * i : NV * CHUNKS * (i + 1), :],
-                    in_=vec.rearrange("n (c p) -> (n c) p", p=P),
-                )
-
-        def load_rows(src, name):
-            tiles = []
-            for h in range(HALVES):
-                t = loads.tile([P, NV * D], BF16, name="%s%d" % (name, h))
-                nc.sync.dma_start(
-                    out=t[:], in_=src[h * P : (h + 1) * P].rearrange("b n d -> b (n d)")
-                )
-                tiles.append(t)
-            return tiles
+        def load_rows(src, n, name):
+            t = loads.tile([P, HALVES * D], BF16, name="%s%d" % (name, n))
+            nc.sync.dma_start(
+                out=t[:].rearrange("p (h d) -> p h d", h=HALVES),
+                in_=src[:, n, :].rearrange("(h p) d -> p h d", p=P),
+            )
+            return t
 
         def load_w1(n):
             t = loads.tile([P, PACK, D], BF16, name="w1_raw%d" % n)
@@ -72,55 +73,33 @@ def tile_variableselectionnetwork_pb_kernel(
             nc.sync.dma_start(out=t[:], in_=w[n].rearrange("(t p) c -> p t c", p=P))
             return t
 
-        w1_raw, w4_raw, w5_raw = {}, {}, {}
-        load_bias_rows()
-        w1_raw[0] = load_w1(0)
-        hv_sb = load_rows(hv, "hv")
-        w4_raw[0] = load_w45(vW4, 0, "w4")
-        w5_raw[0] = load_w45(vW5, 0, "w5")
-        w1_raw[1] = load_w1(1)
-        w4_raw[1] = load_w45(vW4, 1, "w4")
-        w5_raw[1] = load_w45(vW5, 1, "w5")
-        w1_raw[2] = load_w1(2)
-        x_sb = load_rows(x, "x")
-        w4_raw[2] = load_w45(vW4, 2, "w4")
-        w5_raw[2] = load_w45(vW5, 2, "w5")
-        sel_sb = load_rows(sel_w, "sel")
-        w1_raw[3] = load_w1(3)
-        w4_raw[3] = load_w45(vW4, 3, "w4")
-        w5_raw[3] = load_w45(vW5, 3, "w5")
+        w1_raw, hv_sb, w4_raw, w5_raw, x_sb, sel_sb = [], [], [], [], [], []
+        for n in range(NV):
+            w1_raw.append(load_w1(n))
+            hv_sb.append(load_rows(hv, n, "hv"))
+            w4_raw.append(load_w45(vW4, n, "w4"))
+            w5_raw.append(load_w45(vW5, n, "w5"))
+            x_sb.append(load_rows(x, n, "x"))
+            sel_sb.append(load_rows(sel_w, n, "sel"))
 
-        ident = consts.tile([P, P], F32)
-        make_identity(nc, ident[:])
         ident_bf16 = consts.tile([P, P], BF16)
         make_identity(nc, ident_bf16[:])
+        ident = consts.tile([P, P], F32)
+        make_identity(nc, ident[:])
         minus_half = consts.tile([P, HALVES], F32)
         nc.gpsimd.memset(minus_half[:], -0.5)
 
         table_warm = consts.tile([P, 1], F32)
         nc.scalar.activation(out=table_warm[:], in_=minus_half[:, 0:1], func=ACT.Sigmoid)
 
-        bias_cols = consts.tile([P, BIAS_VECTORS * NV * CHUNKS], F32)
-        norm_cols = consts.tile([P, NORM_VECTORS * NV * CHUNKS], BF16)
+        vector_cols = consts.tile([P, P], F32)
+        cols_ps = psum_stage1.tile([P, P], BF16, tag="stage1")
+        nc.tensor.transpose(cols_ps[:], vector_rows[:], ident_bf16[:])
+        nc.vector.tensor_copy(out=vector_cols[:], in_=cols_ps[:])
 
-        def bias_col(i, n, c):
+        def vector_col(i, n, c):
             j = NV * CHUNKS * i + CHUNKS * n + c
-            return bias_cols[:, j : j + 1]
-
-        def spread_over_partitions(i, name):
-            spread = consts.tile([P, NV * D], BF16, name=name)
-            blocks_per_bank = 2 * D // P
-            for bank in range(NV * CHUNKS // blocks_per_bank):
-                spread_ps = psum_gate.tile([P, 2 * D], BF16, tag="gate")
-                for b in range(blocks_per_bank):
-                    j = NV * CHUNKS * i + blocks_per_bank * bank + b
-                    nc.tensor.transpose(
-                        spread_ps[:, b * P : (b + 1) * P],
-                        norm_cols[:, j : j + 1].to_broadcast([P, P]),
-                        ident_bf16[:],
-                    )
-                nc.scalar.copy(out=spread[:, bank * 2 * D : (bank + 1) * 2 * D], in_=spread_ps[:])
-            return spread
+            return vector_cols[:, j : j + 1]
 
         row_sum = consts.tile([P, NV * HALVES], F32)
         sq_sum = consts.tile([P, NV * HALVES], F32)
@@ -128,16 +107,15 @@ def tile_variableselectionnetwork_pb_kernel(
         var_eps = consts.tile([P, NV * HALVES], F32)
         rstd = consts.tile([P, NV * HALVES], F32)
 
-        acc = [consts.tile([P, D], F32, name="acc%d" % h) for h in range(HALVES)]
+        out_ps = [psum_out.tile([P, D], F32, name="out_ps%d" % h) for h in range(HALVES)]
 
         def quantise_weight(raw, name, n):
             grouped = staging.tile([P, D, PACK], BF16, tag="grouped", align_bytes=64)
             dst = grouped[:].rearrange("p (c i) t -> p c t i", i=4)
             src = raw[:].rearrange("p t (c i) -> p c t i", i=4)
-            if n == 0 or name == "w1":
-                nc.vector.tensor_copy(out=dst, in_=src)
-            else:
-                nc.scalar.copy(out=dst, in_=src)
+            split = VECTOR_COLS // 4
+            nc.vector.tensor_copy(out=dst[:, :split], in_=src[:, :split])
+            nc.scalar.copy(out=dst[:, split:], in_=src[:, split:])
             codes = quantised.tile([P, D], U32, name="%s_codes%d" % (name, n), align_bytes=64)
             scales = quantised.tile([P, D], U8, name="%s_scales%d" % (name, n), align_bytes=64)
             nc.vector.quantize_mx(
@@ -152,10 +130,10 @@ def tile_variableselectionnetwork_pb_kernel(
             hvT_ps = psum_stage1.tile([P, 2, B], F32, tag="stage1")
             for u in range(2):
                 for h in range(HALVES):
-                    first = n * words_per_row + u * P
+                    first = h * words_per_row + u * P
                     nc.tensor.transpose(
                         hvT_ps[:, u, h * P : (h + 1) * P],
-                        hv_sb[h][:].bitcast(F32)[:, first : first + P],
+                        hv_sb[n][:].bitcast(F32)[:, first : first + P],
                         ident[:],
                     )
             grouped = staging.tile([P, B * PACK], BF16, tag="hv_grouped", align_bytes=64)
@@ -184,11 +162,11 @@ def tile_variableselectionnetwork_pb_kernel(
                         start=True,
                         stop=True,
                     )
-                first = CHUNKS * n
+                first = NV * CHUNKS * VB1 + CHUNKS * n
                 nc.vector.tensor_tensor(
                     out=grouped[:, rows, :],
                     in0=e1_ps[:].rearrange("p t b -> p b t"),
-                    in1=bias_cols[:, first : first + PACK].unsqueeze(1).to_broadcast([P, P, PACK]),
+                    in1=vector_cols[:, first : first + PACK].unsqueeze(1).to_broadcast([P, P, PACK]),
                     op=ALU.add,
                 )
             codes = staging.tile([P, B], U32, tag="e1_codes", align_bytes=64)
@@ -201,48 +179,45 @@ def tile_variableselectionnetwork_pb_kernel(
             return codes, scales
 
         def gate(n, e1_q, w4_q, w5_q):
-            gvT = work.tile([P, CHUNKS, B], F32, tag="gvT", bufs=2)
-            for pair in range(CHUNKS // 2):
-                banks = []
-                for w_q in (w4_q, w5_q):
-                    g_ps = psum_gate.tile([P, 2, B], F32, tag="gate")
-                    for i in range(2):
-                        c = 2 * pair + i
-                        feats = slice(c * P, (c + 1) * P)
-                        nc.tensor.matmul_mx(
-                            out=g_ps[:, i, :],
-                            lhsT=w_q[0][:, feats].bitcast(FP8X4),
-                            lhsT_scale=w_q[1][:, feats],
-                            rhs=e1_q[0][:].bitcast(FP8X4),
-                            rhs_scale=e1_q[1][:],
-                            start=True,
-                            stop=True,
-                        )
-                    banks.append(g_ps)
-                sig = work.tile([P, 2, B], F32, tag="sig")
-                for i in range(2):
-                    c = 2 * pair + i
-                    nc.scalar.activation(
-                        out=sig[:, i, :], in_=banks[0][:, i, :], func=ACT.Sigmoid, bias=bias_col(1, n, c)
+            gvT = work.tile([P, CHUNKS, B], F32, tag="gvT", bufs=NV)
+            for c in range(CHUNKS):
+                feats = slice(c * P, (c + 1) * P)
+                g_ps = psum_gate.tile([P, 2, B], F32, tag="gate")
+                for i, w_q in enumerate((w4_q, w5_q)):
+                    nc.tensor.matmul_mx(
+                        out=g_ps[:, i, :],
+                        lhsT=w_q[0][:, feats].bitcast(FP8X4),
+                        lhsT_scale=w_q[1][:, feats],
+                        rhs=e1_q[0][:].bitcast(FP8X4),
+                        rhs_scale=e1_q[1][:],
+                        start=True,
+                        stop=True,
                     )
-                    nc.vector.scalar_tensor_tensor(
-                        out=gvT[:, c, :],
-                        in0=banks[1][:, i, :],
-                        scalar=bias_col(2, n, c),
-                        in1=sig[:, i, :],
-                        op0=ALU.add,
-                        op1=ALU.mult,
-                    )
+                sig = work.tile([P, B], F32, tag="sig")
+                nc.scalar.activation(
+                    out=sig[:], in_=g_ps[:, 0, :], func=ACT.Sigmoid, bias=vector_col(VB4, n, c)
+                )
+                nc.vector.scalar_tensor_tensor(
+                    out=gvT[:, c, :],
+                    in0=g_ps[:, 1, :],
+                    scalar=vector_col(VB5, n, c),
+                    in1=sig[:],
+                    op0=ALU.add,
+                    op1=ALU.mult,
+                )
             return gvT
 
-        def residual_and_statistics(n, gvT):
-            feats = slice(n * D, (n + 1) * D)
+        def residual_and_mean(n, gvT):
             cols = slice(n * HALVES, (n + 1) * HALVES)
             r = []
             for h in range(HALVES):
-                r_ps = psum_rows.tile([P, D], F32, tag="r_ps")
+                r_ps = psum_rows.tile([P, D], F32, tag="rows")
                 nc.tensor.matmul(
-                    out=r_ps[:], lhsT=ident_bf16[:], rhs=x_sb[h][:, feats], start=True, stop=False
+                    out=r_ps[:],
+                    lhsT=ident_bf16[:],
+                    rhs=x_sb[n][:, h * D : (h + 1) * D],
+                    start=True,
+                    stop=False,
                 )
                 for c in range(CHUNKS):
                     nc.tensor.matmul(
@@ -263,9 +238,13 @@ def tile_variableselectionnetwork_pb_kernel(
                 out=neg_mean[:, cols], in0=row_sum[:, cols],
                 scalar1=-1.0 / D, scalar2=0.0, op0=ALU.mult, op1=ALU.add,
             )
+            return r
+
+        def inverse_deviation(n, r):
+            cols = slice(n * HALVES, (n + 1) * HALVES)
             for h in range(HALVES):
                 j = n * HALVES + h
-                squares = work.tile([P, D], BF16, tag="squares")
+                squares = work.tile([P, D], BF16, tag="squares", bufs=2)
                 nc.scalar.activation(
                     out=squares[:], in_=r[h][:], func=ACT.Square,
                     bias=neg_mean[:, j : j + 1], accum_out=sq_sum[:, j : j + 1],
@@ -277,61 +256,89 @@ def tile_variableselectionnetwork_pb_kernel(
             nc.gpsimd.tensor_tensor(
                 out=rstd[:, cols], in0=var_eps[:, cols], in1=minus_half[:], op=ALU.pow
             )
-            return r
 
-        def normalise_and_add(n, r):
-            feats = slice(n * D, (n + 1) * D)
-            scaled, y, weighted = [], [], []
+        def transpose_sel(n):
+            selT_ps = psum_stage1.tile([P, CHUNKS, B], BF16, tag="stage1")
+            for c in range(CHUNKS):
+                for h in range(HALVES):
+                    first = h * D + c * P
+                    nc.tensor.transpose(
+                        selT_ps[:, c, h * P : (h + 1) * P],
+                        sel_sb[n][:, first : first + P],
+                        ident_bf16[:],
+                    )
+            selT = consts.tile([P, CHUNKS, B], BF16, name="selT%d" % n)
+            nc.vector.tensor_copy(out=selT[:], in_=selT_ps[:])
+            return selT
+
+        def normalise(n, r):
+            z = []
             for h in range(HALVES):
                 j = n * HALVES + h
-                t = work.tile([P, D], F32, tag="scaled")
-                nc.vector.scalar_tensor_tensor(
-                    out=t[:], in0=r[h][:], scalar=neg_mean[:, j : j + 1], in1=gamma_bc[:, feats],
+                z_h = work.tile([P, D], F32, tag="z", bufs=NV * HALVES)
+                nc.vector.tensor_scalar(
+                    out=z_h[:], in0=r[h][:],
+                    scalar1=neg_mean[:, j : j + 1], scalar2=rstd[:, j : j + 1],
                     op0=ALU.add, op1=ALU.mult,
                 )
-                scaled.append(t)
-            for h in range(HALVES):
-                j = n * HALVES + h
-                t = work.tile([P, D], F32, tag="y")
-                nc.vector.scalar_tensor_tensor(
-                    out=t[:], in0=scaled[h][:], scalar=rstd[:, j : j + 1], in1=beta_bc[:, feats],
-                    op0=ALU.mult, op1=ALU.add,
+                z.append(z_h)
+            return z
+
+        def scale_shift_and_weigh(n, z, selT):
+            weightedT = work.tile([P, CHUNKS, B], F32, tag="weightedT", bufs=2)
+            for pair in range(CHUNKS // 2):
+                zT_ps = psum_rows.tile([P, 2, B], F32, tag="rows")
+                for i in range(2):
+                    c = 2 * pair + i
+                    for h in range(HALVES):
+                        nc.tensor.transpose(
+                            zT_ps[:, i, h * P : (h + 1) * P], z[h][:, c * P : (c + 1) * P], ident[:]
+                        )
+                yT = work.tile([P, 2, B], F32, tag="yT")
+                for i in range(2):
+                    c = 2 * pair + i
+                    nc.scalar.activation(
+                        out=yT[:, i, :], in_=zT_ps[:, i, :], func=ACT.Identity,
+                        scale=vector_col(VLNG, n, c), bias=vector_col(VLNB, n, c),
+                    )
+                chunks = slice(2 * pair, 2 * pair + 2)
+                nc.vector.tensor_tensor(
+                    out=weightedT[:, chunks, :], in0=yT[:], in1=selT[:, chunks, :], op=ALU.mult
                 )
-                y.append(t)
+            return weightedT
+
+        def add_to_out(n, weightedT):
             for h in range(HALVES):
-                t = acc[h] if n == 0 else work.tile([P, D], F32, name="weighted", tag="weighted")
-                nc.vector.tensor_tensor(out=t[:], in0=y[h][:], in1=sel_sb[h][:, feats], op=ALU.mult)
-                weighted.append(t)
-            if n > 0:
-                for h in range(HALVES):
-                    nc.vector.tensor_tensor(
-                        out=acc[h][:], in0=acc[h][:], in1=weighted[h][:], op=ALU.add
+                for c in range(CHUNKS):
+                    nc.tensor.matmul(
+                        out=out_ps[h][:, c * P : (c + 1) * P],
+                        lhsT=weightedT[:, c, h * P : (h + 1) * P],
+                        rhs=ident[:],
+                        is_transpose=True,
+                        start=(n == 0 and c == 0),
+                        stop=(n == NV - 1 and c == CHUNKS - 1),
                     )
 
-        def products_and_statistics(n):
+        variables = range(NV)
+        gvT = []
+        for n in variables:
             w1_q = quantise_weight(w1_raw[n], "w1", n)
-            e1_q = first_product(n, w1_q, hv_q[n])
+            hv_q = quantise_hv(n)
+            e1_q = first_product(n, w1_q, hv_q)
             w4_q = quantise_weight(w4_raw[n], "w4", n)
             w5_q = quantise_weight(w5_raw[n], "w5", n)
-            gvT = gate(n, e1_q, w4_q, w5_q)
-            return residual_and_statistics(n, gvT)
+            gvT.append(gate(n, e1_q, w4_q, w5_q))
+        r = [residual_and_mean(n, gvT[n]) for n in variables]
+        for n in variables:
+            inverse_deviation(n, r[n])
+        selT = [transpose_sel(n) for n in variables]
+        z = [normalise(n, r[n]) for n in variables]
+        weightedT = [scale_shift_and_weigh(n, z[n], selT[n]) for n in variables]
+        for n in variables:
+            add_to_out(n, weightedT[n])
 
-        cols_ps = psum_stage1.tile([P, P], BF16, tag="stage1")
-        nc.tensor.transpose(cols_ps[:], bias_rows[:], ident_bf16[:])
-        first_norm_col = BIAS_VECTORS * NV * CHUNKS
-        nc.vector.tensor_copy(out=bias_cols[:], in_=cols_ps[:, 0:first_norm_col])
-        nc.vector.tensor_copy(
-            out=norm_cols[:],
-            in_=cols_ps[:, first_norm_col : first_norm_col + NORM_VECTORS * NV * CHUNKS],
-        )
-        hv_q = [quantise_hv(n) for n in range(NV)]
-        r = [products_and_statistics(0)]
-        gamma_bc = spread_over_partitions(0, "gamma_bc")
-        beta_bc = spread_over_partitions(1, "beta_bc")
-        for n in range(1, NV):
-            r.append(products_and_statistics(n))
-        for n in range(NV):
-            normalise_and_add(n, r[n])
-
+        out_sb = [consts.tile([P, D], F32, name="out_sb%d" % h) for h in range(HALVES)]
+        nc.scalar.copy(out=out_sb[0][:], in_=out_ps[0][:])
+        nc.vector.tensor_copy(out=out_sb[1][:], in_=out_ps[1][:])
         for h in range(HALVES):
-            nc.sync.dma_start(out=out[h * P : (h + 1) * P, :], in_=acc[h][:])
+            nc.sync.dma_start(out=out[h * P : (h + 1) * P, :], in_=out_sb[h][:])

@@ -19,12 +19,9 @@ D = 512
 HALVES = B // P
 CHUNKS = D // P
 EPS = 1e-5
-VB1 = 0
-VB4 = 1
-VB5 = 2
-VLNG = 3
-VLNB = 4
-VECTOR_COLS = 256
+BIAS_VECTORS = 3
+NORM_VECTORS = 2
+VECTOR_COLS = 192
 
 FLOPS = 3 * NV * 2 * B * D * D
 
@@ -40,25 +37,28 @@ def tile_variableselectionnetwork_pb_kernel(
         staging = ctx.enter_context(tc.tile_pool(name="staging", bufs=3))
         work = ctx.enter_context(tc.tile_pool(name="work", bufs=4))
         psum_stage1 = ctx.enter_context(tc.psum_pool(name="psum_stage1", bufs=2))
-        psum_gate = ctx.enter_context(tc.psum_pool(name="psum_gate", bufs=2))
+        psum_gate = ctx.enter_context(tc.psum_pool(name="psum_gate", bufs=4))
         psum_rows = ctx.enter_context(tc.psum_pool(name="psum_rows", bufs=2))
-        psum_out = ctx.enter_context(tc.psum_pool(name="psum_out", bufs=1))
 
-        vector_rows = consts.tile([P, P], BF16)
-        nc.vector.memset(vector_rows[:], 0.0)
-        for i, vec in enumerate((vb1, vb4, vb5, vlng, vlnb)):
-            nc.sync.dma_start(
-                out=vector_rows[NV * CHUNKS * i : NV * CHUNKS * (i + 1), :],
-                in_=vec.rearrange("n (c p) -> (n c) p", p=P),
-            )
+        bias_rows = consts.tile([P, P], BF16)
+        nc.vector.memset(bias_rows[:], 0.0)
 
-        def load_rows(src, n, name):
-            t = loads.tile([P, HALVES * D], BF16, name="%s%d" % (name, n))
-            nc.sync.dma_start(
-                out=t[:].rearrange("p (h d) -> p h d", h=HALVES),
-                in_=src[:, n, :].rearrange("(h p) d -> p h d", p=P),
-            )
-            return t
+        def load_bias_rows():
+            for i, vec in enumerate((vb1, vb4, vb5, vlng, vlnb)):
+                nc.sync.dma_start(
+                    out=bias_rows[NV * CHUNKS * i : NV * CHUNKS * (i + 1), :],
+                    in_=vec.rearrange("n (c p) -> (n c) p", p=P),
+                )
+
+        def load_rows(src, name):
+            tiles = []
+            for h in range(HALVES):
+                t = loads.tile([P, NV * D], BF16, name="%s%d" % (name, h))
+                nc.sync.dma_start(
+                    out=t[:], in_=src[h * P : (h + 1) * P].rearrange("b n d -> b (n d)")
+                )
+                tiles.append(t)
+            return tiles
 
         def load_w1(n):
             t = loads.tile([P, PACK, D], BF16, name="w1_raw%d" % n)
@@ -73,33 +73,55 @@ def tile_variableselectionnetwork_pb_kernel(
             nc.sync.dma_start(out=t[:], in_=w[n].rearrange("(t p) c -> p t c", p=P))
             return t
 
-        w1_raw, hv_sb, w4_raw, w5_raw, x_sb, sel_sb = [], [], [], [], [], []
-        for n in range(NV):
-            w1_raw.append(load_w1(n))
-            hv_sb.append(load_rows(hv, n, "hv"))
-            w4_raw.append(load_w45(vW4, n, "w4"))
-            w5_raw.append(load_w45(vW5, n, "w5"))
-            x_sb.append(load_rows(x, n, "x"))
-            sel_sb.append(load_rows(sel_w, n, "sel"))
+        w1_raw, w4_raw, w5_raw = {}, {}, {}
+        load_bias_rows()
+        w1_raw[0] = load_w1(0)
+        hv_sb = load_rows(hv, "hv")
+        w4_raw[0] = load_w45(vW4, 0, "w4")
+        w5_raw[0] = load_w45(vW5, 0, "w5")
+        w1_raw[1] = load_w1(1)
+        w4_raw[1] = load_w45(vW4, 1, "w4")
+        w5_raw[1] = load_w45(vW5, 1, "w5")
+        w1_raw[2] = load_w1(2)
+        x_sb = load_rows(x, "x")
+        w4_raw[2] = load_w45(vW4, 2, "w4")
+        w5_raw[2] = load_w45(vW5, 2, "w5")
+        sel_sb = load_rows(sel_w, "sel")
+        w1_raw[3] = load_w1(3)
+        w4_raw[3] = load_w45(vW4, 3, "w4")
+        w5_raw[3] = load_w45(vW5, 3, "w5")
 
-        ident_bf16 = consts.tile([P, P], BF16)
-        make_identity(nc, ident_bf16[:])
         ident = consts.tile([P, P], F32)
         make_identity(nc, ident[:])
+        ident_bf16 = consts.tile([P, P], BF16)
+        make_identity(nc, ident_bf16[:])
         minus_half = consts.tile([P, HALVES], F32)
         nc.gpsimd.memset(minus_half[:], -0.5)
 
         table_warm = consts.tile([P, 1], F32)
         nc.scalar.activation(out=table_warm[:], in_=minus_half[:, 0:1], func=ACT.Sigmoid)
 
-        vector_cols = consts.tile([P, P], F32)
-        cols_ps = psum_stage1.tile([P, P], BF16, tag="stage1")
-        nc.tensor.transpose(cols_ps[:], vector_rows[:], ident_bf16[:])
-        nc.vector.tensor_copy(out=vector_cols[:], in_=cols_ps[:])
+        bias_cols = consts.tile([P, BIAS_VECTORS * NV * CHUNKS], F32)
+        norm_cols = consts.tile([P, NORM_VECTORS * NV * CHUNKS], BF16)
 
-        def vector_col(i, n, c):
+        def bias_col(i, n, c):
             j = NV * CHUNKS * i + CHUNKS * n + c
-            return vector_cols[:, j : j + 1]
+            return bias_cols[:, j : j + 1]
+
+        def spread_over_partitions(i, name):
+            spread = consts.tile([P, NV * D], BF16, name=name)
+            blocks_per_bank = 2 * D // P
+            for bank in range(NV * CHUNKS // blocks_per_bank):
+                spread_ps = psum_gate.tile([P, 2 * D], BF16, tag="gate")
+                for b in range(blocks_per_bank):
+                    j = NV * CHUNKS * i + blocks_per_bank * bank + b
+                    nc.tensor.transpose(
+                        spread_ps[:, b * P : (b + 1) * P],
+                        norm_cols[:, j : j + 1].to_broadcast([P, P]),
+                        ident_bf16[:],
+                    )
+                nc.scalar.copy(out=spread[:, bank * 2 * D : (bank + 1) * 2 * D], in_=spread_ps[:])
+            return spread
 
         row_sum = consts.tile([P, NV * HALVES], F32)
         sq_sum = consts.tile([P, NV * HALVES], F32)
@@ -107,7 +129,7 @@ def tile_variableselectionnetwork_pb_kernel(
         var_eps = consts.tile([P, NV * HALVES], F32)
         rstd = consts.tile([P, NV * HALVES], F32)
 
-        out_ps = [psum_out.tile([P, D], F32, name="out_ps%d" % h) for h in range(HALVES)]
+        acc = [consts.tile([P, D], F32, name="acc%d" % h) for h in range(HALVES)]
 
         def quantise_weight(raw, name, n):
             grouped = staging.tile([P, D, PACK], BF16, tag="grouped", align_bytes=64)
@@ -130,10 +152,10 @@ def tile_variableselectionnetwork_pb_kernel(
             hvT_ps = psum_stage1.tile([P, 2, B], F32, tag="stage1")
             for u in range(2):
                 for h in range(HALVES):
-                    first = h * words_per_row + u * P
+                    first = n * words_per_row + u * P
                     nc.tensor.transpose(
                         hvT_ps[:, u, h * P : (h + 1) * P],
-                        hv_sb[n][:].bitcast(F32)[:, first : first + P],
+                        hv_sb[h][:].bitcast(F32)[:, first : first + P],
                         ident[:],
                     )
             grouped = staging.tile([P, B * PACK], BF16, tag="hv_grouped", align_bytes=64)
@@ -162,11 +184,11 @@ def tile_variableselectionnetwork_pb_kernel(
                         start=True,
                         stop=True,
                     )
-                first = NV * CHUNKS * VB1 + CHUNKS * n
+                first = CHUNKS * n
                 nc.vector.tensor_tensor(
                     out=grouped[:, rows, :],
                     in0=e1_ps[:].rearrange("p t b -> p b t"),
-                    in1=vector_cols[:, first : first + PACK].unsqueeze(1).to_broadcast([P, P, PACK]),
+                    in1=bias_cols[:, first : first + PACK].unsqueeze(1).to_broadcast([P, P, PACK]),
                     op=ALU.add,
                 )
             codes = staging.tile([P, B], U32, tag="e1_codes", align_bytes=64)
@@ -179,45 +201,48 @@ def tile_variableselectionnetwork_pb_kernel(
             return codes, scales
 
         def gate(n, e1_q, w4_q, w5_q):
-            gvT = work.tile([P, CHUNKS, B], F32, tag="gvT", bufs=NV)
-            for c in range(CHUNKS):
-                feats = slice(c * P, (c + 1) * P)
-                g_ps = psum_gate.tile([P, 2, B], F32, tag="gate")
-                for i, w_q in enumerate((w4_q, w5_q)):
-                    nc.tensor.matmul_mx(
-                        out=g_ps[:, i, :],
-                        lhsT=w_q[0][:, feats].bitcast(FP8X4),
-                        lhsT_scale=w_q[1][:, feats],
-                        rhs=e1_q[0][:].bitcast(FP8X4),
-                        rhs_scale=e1_q[1][:],
-                        start=True,
-                        stop=True,
+            gvT = work.tile([P, CHUNKS, B], F32, tag="gvT", bufs=2)
+            for pair in range(CHUNKS // 2):
+                banks = []
+                for w_q in (w4_q, w5_q):
+                    g_ps = psum_gate.tile([P, 2, B], F32, tag="gate")
+                    for i in range(2):
+                        c = 2 * pair + i
+                        feats = slice(c * P, (c + 1) * P)
+                        nc.tensor.matmul_mx(
+                            out=g_ps[:, i, :],
+                            lhsT=w_q[0][:, feats].bitcast(FP8X4),
+                            lhsT_scale=w_q[1][:, feats],
+                            rhs=e1_q[0][:].bitcast(FP8X4),
+                            rhs_scale=e1_q[1][:],
+                            start=True,
+                            stop=True,
+                        )
+                    banks.append(g_ps)
+                sig = work.tile([P, 2, B], F32, tag="sig")
+                for i in range(2):
+                    c = 2 * pair + i
+                    nc.scalar.activation(
+                        out=sig[:, i, :], in_=banks[0][:, i, :], func=ACT.Sigmoid, bias=bias_col(1, n, c)
                     )
-                sig = work.tile([P, B], F32, tag="sig")
-                nc.scalar.activation(
-                    out=sig[:], in_=g_ps[:, 0, :], func=ACT.Sigmoid, bias=vector_col(VB4, n, c)
-                )
-                nc.vector.scalar_tensor_tensor(
-                    out=gvT[:, c, :],
-                    in0=g_ps[:, 1, :],
-                    scalar=vector_col(VB5, n, c),
-                    in1=sig[:],
-                    op0=ALU.add,
-                    op1=ALU.mult,
-                )
+                    nc.vector.scalar_tensor_tensor(
+                        out=gvT[:, c, :],
+                        in0=banks[1][:, i, :],
+                        scalar=bias_col(2, n, c),
+                        in1=sig[:, i, :],
+                        op0=ALU.add,
+                        op1=ALU.mult,
+                    )
             return gvT
 
-        def residual_and_mean(n, gvT):
+        def residual_and_statistics(n, gvT):
+            feats = slice(n * D, (n + 1) * D)
             cols = slice(n * HALVES, (n + 1) * HALVES)
             r = []
             for h in range(HALVES):
-                r_ps = psum_rows.tile([P, D], F32, tag="rows")
+                r_ps = psum_rows.tile([P, D], F32, tag="r_ps")
                 nc.tensor.matmul(
-                    out=r_ps[:],
-                    lhsT=ident_bf16[:],
-                    rhs=x_sb[n][:, h * D : (h + 1) * D],
-                    start=True,
-                    stop=False,
+                    out=r_ps[:], lhsT=ident_bf16[:], rhs=x_sb[h][:, feats], start=True, stop=False
                 )
                 for c in range(CHUNKS):
                     nc.tensor.matmul(
@@ -238,13 +263,9 @@ def tile_variableselectionnetwork_pb_kernel(
                 out=neg_mean[:, cols], in0=row_sum[:, cols],
                 scalar1=-1.0 / D, scalar2=0.0, op0=ALU.mult, op1=ALU.add,
             )
-            return r
-
-        def inverse_deviation(n, r):
-            cols = slice(n * HALVES, (n + 1) * HALVES)
             for h in range(HALVES):
                 j = n * HALVES + h
-                squares = work.tile([P, D], BF16, tag="squares", bufs=2)
+                squares = work.tile([P, D], BF16, tag="squares")
                 nc.scalar.activation(
                     out=squares[:], in_=r[h][:], func=ACT.Square,
                     bias=neg_mean[:, j : j + 1], accum_out=sq_sum[:, j : j + 1],
@@ -256,89 +277,59 @@ def tile_variableselectionnetwork_pb_kernel(
             nc.gpsimd.tensor_tensor(
                 out=rstd[:, cols], in0=var_eps[:, cols], in1=minus_half[:], op=ALU.pow
             )
+            return r
 
-        def transpose_sel(n):
-            selT_ps = psum_stage1.tile([P, CHUNKS, B], BF16, tag="stage1")
-            for c in range(CHUNKS):
-                for h in range(HALVES):
-                    first = h * D + c * P
-                    nc.tensor.transpose(
-                        selT_ps[:, c, h * P : (h + 1) * P],
-                        sel_sb[n][:, first : first + P],
-                        ident_bf16[:],
-                    )
-            selT = consts.tile([P, CHUNKS, B], BF16, name="selT%d" % n)
-            nc.vector.tensor_copy(out=selT[:], in_=selT_ps[:])
-            return selT
-
-        def normalise(n, r):
-            z = []
+        def normalise_and_add(n, r):
+            feats = slice(n * D, (n + 1) * D)
+            scaled, y, weighted = [], [], []
             for h in range(HALVES):
                 j = n * HALVES + h
-                z_h = work.tile([P, D], F32, tag="z", bufs=NV * HALVES)
-                nc.vector.tensor_scalar(
-                    out=z_h[:], in0=r[h][:],
-                    scalar1=neg_mean[:, j : j + 1], scalar2=rstd[:, j : j + 1],
+                t = work.tile([P, D], F32, tag="scaled")
+                nc.vector.scalar_tensor_tensor(
+                    out=t[:], in0=r[h][:], scalar=neg_mean[:, j : j + 1], in1=gamma_bc[:, feats],
                     op0=ALU.add, op1=ALU.mult,
                 )
-                z.append(z_h)
-            return z
-
-        def scale_shift_and_weigh(n, z, selT):
-            weightedT = work.tile([P, CHUNKS, B], F32, tag="weightedT", bufs=2)
-            for pair in range(CHUNKS // 2):
-                zT_ps = psum_rows.tile([P, 2, B], F32, tag="rows")
-                for i in range(2):
-                    c = 2 * pair + i
-                    for h in range(HALVES):
-                        nc.tensor.transpose(
-                            zT_ps[:, i, h * P : (h + 1) * P], z[h][:, c * P : (c + 1) * P], ident[:]
-                        )
-                yT = work.tile([P, 2, B], F32, tag="yT")
-                for i in range(2):
-                    c = 2 * pair + i
-                    nc.scalar.activation(
-                        out=yT[:, i, :], in_=zT_ps[:, i, :], func=ACT.Identity,
-                        scale=vector_col(VLNG, n, c), bias=vector_col(VLNB, n, c),
-                    )
-                chunks = slice(2 * pair, 2 * pair + 2)
-                nc.vector.tensor_tensor(
-                    out=weightedT[:, chunks, :], in0=yT[:], in1=selT[:, chunks, :], op=ALU.mult
-                )
-            return weightedT
-
-        def add_to_out(n, weightedT):
+                scaled.append(t)
             for h in range(HALVES):
-                for c in range(CHUNKS):
-                    nc.tensor.matmul(
-                        out=out_ps[h][:, c * P : (c + 1) * P],
-                        lhsT=weightedT[:, c, h * P : (h + 1) * P],
-                        rhs=ident[:],
-                        is_transpose=True,
-                        start=(n == 0 and c == 0),
-                        stop=(n == NV - 1 and c == CHUNKS - 1),
+                j = n * HALVES + h
+                t = work.tile([P, D], F32, tag="y")
+                nc.vector.scalar_tensor_tensor(
+                    out=t[:], in0=scaled[h][:], scalar=rstd[:, j : j + 1], in1=beta_bc[:, feats],
+                    op0=ALU.mult, op1=ALU.add,
+                )
+                y.append(t)
+            for h in range(HALVES):
+                t = acc[h] if n == 0 else work.tile([P, D], F32, name="weighted", tag="weighted")
+                nc.vector.tensor_tensor(out=t[:], in0=y[h][:], in1=sel_sb[h][:, feats], op=ALU.mult)
+                weighted.append(t)
+            if n > 0:
+                for h in range(HALVES):
+                    nc.vector.tensor_tensor(
+                        out=acc[h][:], in0=acc[h][:], in1=weighted[h][:], op=ALU.add
                     )
 
-        variables = range(NV)
-        gvT = []
-        for n in variables:
+        def products_and_statistics(n):
             w1_q = quantise_weight(w1_raw[n], "w1", n)
-            hv_q = quantise_hv(n)
-            e1_q = first_product(n, w1_q, hv_q)
+            e1_q = first_product(n, w1_q, hv_q[n])
             w4_q = quantise_weight(w4_raw[n], "w4", n)
             w5_q = quantise_weight(w5_raw[n], "w5", n)
-            gvT.append(gate(n, e1_q, w4_q, w5_q))
-        r = [residual_and_mean(n, gvT[n]) for n in variables]
-        for n in variables:
-            inverse_deviation(n, r[n])
-        selT = [transpose_sel(n) for n in variables]
-        z = [normalise(n, r[n]) for n in variables]
-        weightedT = [scale_shift_and_weigh(n, z[n], selT[n]) for n in variables]
-        for n in variables:
-            add_to_out(n, weightedT[n])
+            gvT = gate(n, e1_q, w4_q, w5_q)
+            return residual_and_statistics(n, gvT)
 
-        out_sb = [consts.tile([P, D], F32, name="out_sb%d" % h) for h in range(HALVES)]
-        nc.scalar.copy(out=out_sb[0][:], in_=out_ps[0][:])
-        nc.vector.tensor_copy(out=out_sb[1][:], in_=out_ps[1][:])
+        cols_ps = psum_stage1.tile([P, P], BF16, tag="stage1")
+        nc.tensor.transpose(cols_ps[:], bias_rows[:], ident_bf16[:])
+        first_norm_col = BIAS_VECTORS * NV * CHUNKS
+        nc.vector.tensor_copy(out=bias_cols[:], in_=cols_ps[:, 0:first_norm_col])
+        nc.vector.tensor_copy(
+            out=norm_cols[:],
+            in_=cols_ps[:, first_norm_col : first_norm_col + NORM_VECTORS * NV * CHUNKS],
+        )
+        gamma_bc = spread_over_partitions(0, "gamma_bc")
+        beta_bc = spread_over_partitions(1, "beta_bc")
+        hv_q = [quantise_hv(n) for n in range(NV)]
+        r = [products_and_statistics(n) for n in range(NV)]
+        for n in range(NV):
+            normalise_and_add(n, r[n])
+
         for h in range(HALVES):
-            nc.sync.dma_start(out=out[h * P : (h + 1) * P, :], in_=out_sb[h][:])
+            nc.sync.dma_start(out=out[h * P : (h + 1) * P, :], in_=acc[h][:])

from contextlib import ExitStack

import concourse.mybir as mybir
from concourse.masks import make_identity

F32 = mybir.dt.float32
BF16 = mybir.dt.bfloat16
U32 = mybir.dt.uint32
U8 = mybir.dt.uint8
FP8X4 = mybir.dt.float8_e4m3fn_x4
ALU = mybir.AluOpType
ACT = mybir.ActivationFunctionType

P = 128
PACK = 4
B = 256
NV = 4
D = 512
HALVES = B // P
CHUNKS = D // P
EPS = 1e-5
BIAS_VECTORS = 3
NORM_VECTORS = 2
VECTOR_COLS = 192

FLOPS = 3 * NV * 2 * B * D * D


def tile_variableselectionnetwork_pb_kernel(
    tc, hv, x, sel_w, vW1, vb1, vW4, vb4, vW5, vb5, vlng, vlnb, out
):
    nc = tc.nc
    with ExitStack() as ctx:
        consts = ctx.enter_context(tc.tile_pool(name="consts", bufs=1))
        loads = ctx.enter_context(tc.tile_pool(name="loads", bufs=1))
        quantised = ctx.enter_context(tc.tile_pool(name="quantised", bufs=1))
        staging = ctx.enter_context(tc.tile_pool(name="staging", bufs=3))
        work = ctx.enter_context(tc.tile_pool(name="work", bufs=4))
        psum_stage1 = ctx.enter_context(tc.psum_pool(name="psum_stage1", bufs=2))
        psum_gate = ctx.enter_context(tc.psum_pool(name="psum_gate", bufs=4))
        psum_rows = ctx.enter_context(tc.psum_pool(name="psum_rows", bufs=2))

        bias_rows = consts.tile([P, P], BF16)
        nc.vector.memset(bias_rows[:], 0.0)

        def load_bias_rows():
            for i, vec in enumerate((vb1, vb4, vb5, vlng, vlnb)):
                nc.sync.dma_start(
                    out=bias_rows[NV * CHUNKS * i : NV * CHUNKS * (i + 1), :],
                    in_=vec.rearrange("n (c p) -> (n c) p", p=P),
                )

        def load_rows(src, name):
            tiles = []
            for h in range(HALVES):
                t = loads.tile([P, NV * D], BF16, name="%s%d" % (name, h))
                nc.sync.dma_start(
                    out=t[:], in_=src[h * P : (h + 1) * P].rearrange("b n d -> b (n d)")
                )
                tiles.append(t)
            return tiles

        def load_w1(n):
            t = loads.tile([P, PACK, D], BF16, name="w1_raw%d" % n)
            nc.sync.dma_start(
                out=t[:].rearrange("q (u e) c -> q u e c", u=2),
                in_=vW1[n].rearrange("(u q e) c -> q u e c", u=2, e=2),
            )
            return t

        def load_w45(w, n, name):
            t = loads.tile([P, PACK, D], BF16, name="%s_raw%d" % (name, n))
            nc.sync.dma_start(out=t[:], in_=w[n].rearrange("(t p) c -> p t c", p=P))
            return t

        w1_raw, w4_raw, w5_raw = {}, {}, {}
        load_bias_rows()
        w1_raw[0] = load_w1(0)
        hv_sb = load_rows(hv, "hv")
        w4_raw[0] = load_w45(vW4, 0, "w4")
        w5_raw[0] = load_w45(vW5, 0, "w5")
        w1_raw[1] = load_w1(1)
        w4_raw[1] = load_w45(vW4, 1, "w4")
        w5_raw[1] = load_w45(vW5, 1, "w5")
        w1_raw[2] = load_w1(2)
        x_sb = load_rows(x, "x")
        w4_raw[2] = load_w45(vW4, 2, "w4")
        w5_raw[2] = load_w45(vW5, 2, "w5")
        sel_sb = load_rows(sel_w, "sel")
        w1_raw[3] = load_w1(3)
        w4_raw[3] = load_w45(vW4, 3, "w4")
        w5_raw[3] = load_w45(vW5, 3, "w5")

        ident = consts.tile([P, P], F32)
        make_identity(nc, ident[:])
        ident_bf16 = consts.tile([P, P], BF16)
        make_identity(nc, ident_bf16[:])
        minus_half = consts.tile([P, HALVES], F32)
        nc.gpsimd.memset(minus_half[:], -0.5)

        table_warm = consts.tile([P, 1], F32)
        nc.scalar.activation(out=table_warm[:], in_=minus_half[:, 0:1], func=ACT.Sigmoid)

        bias_cols = consts.tile([P, BIAS_VECTORS * NV * CHUNKS], F32)
        norm_cols = consts.tile([P, NORM_VECTORS * NV * CHUNKS], BF16)

        def bias_col(i, n, c):
            j = NV * CHUNKS * i + CHUNKS * n + c
            return bias_cols[:, j : j + 1]

        def spread_over_partitions(i, name):
            spread = consts.tile([P, NV * D], BF16, name=name)
            blocks_per_bank = 2 * D // P
            for bank in range(NV * CHUNKS // blocks_per_bank):
                spread_ps = psum_gate.tile([P, 2 * D], BF16, tag="gate")
                for b in range(blocks_per_bank):
                    j = NV * CHUNKS * i + blocks_per_bank * bank + b
                    nc.tensor.transpose(
                        spread_ps[:, b * P : (b + 1) * P],
                        norm_cols[:, j : j + 1].to_broadcast([P, P]),
                        ident_bf16[:],
                    )
                nc.scalar.copy(out=spread[:, bank * 2 * D : (bank + 1) * 2 * D], in_=spread_ps[:])
            return spread

        row_sum = consts.tile([P, NV * HALVES], F32)
        sq_sum = consts.tile([P, NV * HALVES], F32)
        neg_mean = consts.tile([P, NV * HALVES], F32)
        var_eps = consts.tile([P, NV * HALVES], F32)
        rstd = consts.tile([P, NV * HALVES], F32)

        acc = [consts.tile([P, D], F32, name="acc%d" % h) for h in range(HALVES)]

        def quantise_weight(raw, name, n):
            grouped = staging.tile([P, D, PACK], BF16, tag="grouped", align_bytes=64)
            dst = grouped[:].rearrange("p (c i) t -> p c t i", i=4)
            src = raw[:].rearrange("p t (c i) -> p c t i", i=4)
            split = VECTOR_COLS // 4
            nc.vector.tensor_copy(out=dst[:, :split], in_=src[:, :split])
            nc.scalar.copy(out=dst[:, split:], in_=src[:, split:])
            codes = quantised.tile([P, D], U32, name="%s_codes%d" % (name, n), align_bytes=64)
            scales = quantised.tile([P, D], U8, name="%s_scales%d" % (name, n), align_bytes=64)
            nc.vector.quantize_mx(
                out=codes[:].bitcast(FP8X4),
                scales=scales[:],
                in_=grouped[:].rearrange("p c t -> p (c t)"),
            )
            return codes, scales

        def quantise_hv(n):
            words_per_row = D // 2
            hvT_ps = psum_stage1.tile([P, 2, B], F32, tag="stage1")
            for u in range(2):
                for h in range(HALVES):
                    first = n * words_per_row + u * P
                    nc.tensor.transpose(
                        hvT_ps[:, u, h * P : (h + 1) * P],
                        hv_sb[h][:].bitcast(F32)[:, first : first + P],
                        ident[:],
                    )
            grouped = staging.tile([P, B * PACK], BF16, tag="hv_grouped", align_bytes=64)
            nc.scalar.copy(
                out=grouped[:].bitcast(F32).rearrange("p (b u) -> p b u", u=2),
                in_=hvT_ps[:].rearrange("p u b -> p b u"),
            )
            codes = quantised.tile([P, B], U32, name="hv_codes%d" % n, align_bytes=64)
            scales = quantised.tile([P, B], U8, name="hv_scales%d" % n, align_bytes=64)
            nc.vector.quantize_mx(out=codes[:].bitcast(FP8X4), scales=scales[:], in_=grouped[:])
            return codes, scales

        def first_product(n, w1_q, hv_q):
            grouped = staging.tile([P, B, PACK], BF16, tag="e1_grouped", align_bytes=64)
            for h in range(HALVES):
                rows = slice(h * P, (h + 1) * P)
                e1_ps = psum_stage1.tile([P, PACK, P], F32, tag="stage1")
                for t in range(PACK):
                    feats = slice(t * P, (t + 1) * P)
                    nc.tensor.matmul_mx(
                        out=e1_ps[:, t, :],
                        lhsT=w1_q[0][:, feats].bitcast(FP8X4),
                        lhsT_scale=w1_q[1][:, feats],
                        rhs=hv_q[0][:, rows].bitcast(FP8X4),
                        rhs_scale=hv_q[1][:, rows],
                        start=True,
                        stop=True,
                    )
                first = CHUNKS * n
                nc.vector.tensor_tensor(
                    out=grouped[:, rows, :],
                    in0=e1_ps[:].rearrange("p t b -> p b t"),
                    in1=bias_cols[:, first : first + PACK].unsqueeze(1).to_broadcast([P, P, PACK]),
                    op=ALU.add,
                )
            codes = staging.tile([P, B], U32, tag="e1_codes", align_bytes=64)
            scales = staging.tile([P, B], U8, tag="e1_scales", align_bytes=64)
            nc.vector.quantize_mx(
                out=codes[:].bitcast(FP8X4),
                scales=scales[:],
                in_=grouped[:].rearrange("p b t -> p (b t)"),
            )
            return codes, scales

        def gate(n, e1_q, w4_q, w5_q):
            gvT = work.tile([P, CHUNKS, B], F32, tag="gvT", bufs=2)
            for pair in range(CHUNKS // 2):
                banks = []
                for w_q in (w4_q, w5_q):
                    g_ps = psum_gate.tile([P, 2, B], F32, tag="gate")
                    for i in range(2):
                        c = 2 * pair + i
                        feats = slice(c * P, (c + 1) * P)
                        nc.tensor.matmul_mx(
                            out=g_ps[:, i, :],
                            lhsT=w_q[0][:, feats].bitcast(FP8X4),
                            lhsT_scale=w_q[1][:, feats],
                            rhs=e1_q[0][:].bitcast(FP8X4),
                            rhs_scale=e1_q[1][:],
                            start=True,
                            stop=True,
                        )
                    banks.append(g_ps)
                sig = work.tile([P, 2, B], F32, tag="sig")
                for i in range(2):
                    c = 2 * pair + i
                    nc.scalar.activation(
                        out=sig[:, i, :], in_=banks[0][:, i, :], func=ACT.Sigmoid, bias=bias_col(1, n, c)
                    )
                    nc.vector.scalar_tensor_tensor(
                        out=gvT[:, c, :],
                        in0=banks[1][:, i, :],
                        scalar=bias_col(2, n, c),
                        in1=sig[:, i, :],
                        op0=ALU.add,
                        op1=ALU.mult,
                    )
            return gvT

        def residual_and_statistics(n, gvT):
            feats = slice(n * D, (n + 1) * D)
            cols = slice(n * HALVES, (n + 1) * HALVES)
            r = []
            for h in range(HALVES):
                r_ps = psum_rows.tile([P, D], F32, tag="r_ps")
                nc.tensor.matmul(
                    out=r_ps[:], lhsT=ident_bf16[:], rhs=x_sb[h][:, feats], start=True, stop=False
                )
                for c in range(CHUNKS):
                    nc.tensor.matmul(
                        out=r_ps[:, c * P : (c + 1) * P],
                        lhsT=gvT[:, c, h * P : (h + 1) * P],
                        rhs=ident[:],
                        is_transpose=True,
                        start=False,
                        stop=(c == CHUNKS - 1),
                    )
                r_h = work.tile([P, D], F32, tag="r", bufs=NV * HALVES)
                j = n * HALVES + h
                nc.scalar.activation(
                    out=r_h[:], in_=r_ps[:], func=ACT.Identity, accum_out=row_sum[:, j : j + 1]
                )
                r.append(r_h)
            nc.gpsimd.tensor_scalar(
                out=neg_mean[:, cols], in0=row_sum[:, cols],
                scalar1=-1.0 / D, scalar2=0.0, op0=ALU.mult, op1=ALU.add,
            )
            for h in range(HALVES):
                j = n * HALVES + h
                squares = work.tile([P, D], BF16, tag="squares")
                nc.scalar.activation(
                    out=squares[:], in_=r[h][:], func=ACT.Square,
                    bias=neg_mean[:, j : j + 1], accum_out=sq_sum[:, j : j + 1],
                )
            nc.gpsimd.tensor_scalar(
                out=var_eps[:, cols], in0=sq_sum[:, cols],
                scalar1=1.0 / D, scalar2=EPS, op0=ALU.mult, op1=ALU.add,
            )
            nc.gpsimd.tensor_tensor(
                out=rstd[:, cols], in0=var_eps[:, cols], in1=minus_half[:], op=ALU.pow
            )
            return r

        def normalise_and_add(n, r):
            feats = slice(n * D, (n + 1) * D)
            scaled, y, weighted = [], [], []
            for h in range(HALVES):
                j = n * HALVES + h
                t = work.tile([P, D], F32, tag="scaled")
                nc.vector.scalar_tensor_tensor(
                    out=t[:], in0=r[h][:], scalar=neg_mean[:, j : j + 1], in1=gamma_bc[:, feats],
                    op0=ALU.add, op1=ALU.mult,
                )
                scaled.append(t)
            for h in range(HALVES):
                j = n * HALVES + h
                t = work.tile([P, D], F32, tag="y")
                nc.vector.scalar_tensor_tensor(
                    out=t[:], in0=scaled[h][:], scalar=rstd[:, j : j + 1], in1=beta_bc[:, feats],
                    op0=ALU.mult, op1=ALU.add,
                )
                y.append(t)
            for h in range(HALVES):
                t = acc[h] if n == 0 else work.tile([P, D], F32, name="weighted", tag="weighted")
                nc.vector.tensor_tensor(out=t[:], in0=y[h][:], in1=sel_sb[h][:, feats], op=ALU.mult)
                weighted.append(t)
            if n > 0:
                for h in range(HALVES):
                    nc.vector.tensor_tensor(
                        out=acc[h][:], in0=acc[h][:], in1=weighted[h][:], op=ALU.add
                    )

        def products_and_statistics(n):
            w1_q = quantise_weight(w1_raw[n], "w1", n)
            e1_q = first_product(n, w1_q, hv_q[n])
            w4_q = quantise_weight(w4_raw[n], "w4", n)
            w5_q = quantise_weight(w5_raw[n], "w5", n)
            gvT = gate(n, e1_q, w4_q, w5_q)
            return residual_and_statistics(n, gvT)

        cols_ps = psum_stage1.tile([P, P], BF16, tag="stage1")
        nc.tensor.transpose(cols_ps[:], bias_rows[:], ident_bf16[:])
        first_norm_col = BIAS_VECTORS * NV * CHUNKS
        nc.vector.tensor_copy(out=bias_cols[:], in_=cols_ps[:, 0:first_norm_col])
        nc.vector.tensor_copy(
            out=norm_cols[:],
            in_=cols_ps[:, first_norm_col : first_norm_col + NORM_VECTORS * NV * CHUNKS],
        )
        gamma_bc = spread_over_partitions(0, "gamma_bc")
        beta_bc = spread_over_partitions(1, "beta_bc")
        hv_q = [quantise_hv(n) for n in range(NV)]
        r = [products_and_statistics(n) for n in range(NV)]
        for n in range(NV):
            normalise_and_add(n, r[n])

        for h in range(HALVES):
            nc.sync.dma_start(out=out[h * P : (h + 1) * P, :], in_=acc[h][:])
